import numpy as np
import ml_dtypes


def mxq(x, axis, fmt="e4m3"):
    dtype, down = {"e4m3": (ml_dtypes.float8_e4m3fn, 7), "e5m2": (ml_dtypes.float8_e5m2, 14)}[fmt]
    v = np.moveaxis(np.asarray(x, np.float32).astype(ml_dtypes.bfloat16).astype(np.float64), axis, -1)
    blocks = v.reshape(v.shape[:-1] + (-1, 32))
    amax = np.abs(blocks).max(-1, keepdims=True)
    byte = np.maximum(np.where(amax > 0, np.frexp(amax)[1] - 1 + 127, 0) - down, 1)
    scale = np.exp2(byte - 127.0)
    codes = (blocks / scale).astype(np.float32).astype(dtype).astype(np.float64)
    return np.moveaxis((codes * scale).reshape(v.shape), -1, axis)


WIDE = False


def mx_kscale(k):
    if not WIDE:
        return np.ones(k)
    levels = np.array([10, -10, 5, -5, 0])
    a = np.random.permutation(np.resize(levels, k // 512 * 4)).reshape(k // 512, 4)
    idx = np.arange(k)
    return np.exp2(a[idx // 512, idx % 128 // 32])


BF16 = ml_dtypes.bfloat16


def bf(x):
    return np.asarray(x, np.float32).astype(BF16)


def f64(x):
    return np.asarray(x).astype(np.float64)


S, B, D, H, F = 512, 2, 1024, 2, 2048
HD = D // H
EPS = 1e-8
ZMAX = 6.0
NTERMS = 120


def rmsnorm(x, w):
    ms = np.mean(x * x, axis=-1, keepdims=True)
    return w * (x / np.sqrt(ms + EPS))


def erf(z):
    a = np.clip(z, -ZMAX, ZMAX)
    y = 2.0 * a * a
    term = a.copy()
    tot = a.copy()
    for n in range(1, NTERMS):
        term *= y
        term *= 1.0 / (2 * n + 1)
        tot += term
    return 2.0 / np.sqrt(np.pi) * np.exp(-a * a) * tot


def gelu_erf(v):
    return 0.5 * v * (1.0 + erf(v / np.sqrt(2.0)))


def setup_inputs():
    s, t = mx_kscale(D), mx_kscale(D)
    return {"h_attn": bf(np.random.standard_normal((B, H, S, HD)) * 0.35 * s.reshape(H, 1, HD)),
            "x": bf(np.random.standard_normal((S, B, D))),
            "out_proj_w": bf(np.random.standard_normal((D, D)) * 2.0 / np.sqrt(D) / s[None, :]),
            "out_proj_b": bf(np.random.standard_normal(D) * 0.2),
            "w_norm2": bf((1.0 + 0.1 * np.random.standard_normal(D)) * t),
            "W1": bf(np.random.standard_normal((F, D)) / np.sqrt(D) / t[None, :]),
            "b1": bf(np.random.standard_normal(F) * 0.3)}


def reference(h_attn, x, out_proj_w, out_proj_b, w_norm2, W1, b1):
    c = f64(h_attn).transpose(2, 0, 1, 3).reshape(S, B, D)
    attn_out = (mxq(c, 2, "e4m3") @ mxq(f64(out_proj_w), 1, "e4m3").T) + f64(out_proj_b)
    x1 = f64(x) + attn_out
    m = rmsnorm(x1, f64(w_norm2))
    g = gelu_erf((mxq(m, 2, "e4m3") @ mxq(f64(W1), 1, "e4m3").T) + f64(b1))
    return x1, g

@@ -1,0 +1,334 @@
+from contextlib import ExitStack
+
+import concourse.mybir as mybir
+from concourse.masks import make_identity
+
+BF16 = mybir.dt.bfloat16
+F32 = mybir.dt.float32
+U32 = mybir.dt.uint32
+U8 = mybir.dt.uint8
+FP8X4 = mybir.dt.float8_e4m3fn_x4
+ALU = mybir.AluOpType
+ACT = mybir.ActivationFunctionType
+
+P = 128
+PACK = 4
+K_PASS = P * PACK
+BANK = 512
+SEQ, BATCH, DIM, HEADS, FF = 512, 2, 1024, 2, 2048
+HEAD_DIM = DIM // HEADS
+PASSES = DIM // K_PASS
+POS = SEQ // P
+TOKEN_TILES = BATCH * POS
+PAIRS = K_PASS // 2
+EPS = 1e-8
+
+FLOPS = 2 * SEQ * BATCH * DIM * (DIM + FF)
+
+
+UNITS_PER_ROUND = 2
+
+
+def tile_transformerblock_pb_kernel(
+    tc, h_attn, x, out_proj_w, out_proj_b, w_norm2, W1, b1, out_0, out_1
+):
+    nc = tc.nc
+    with ExitStack() as stack:
+        const = stack.enter_context(tc.tile_pool(name="const", bufs=1))
+        raw = stack.enter_context(tc.tile_pool(name="raw", bufs=1))
+        keep = stack.enter_context(tc.tile_pool(name="keep", bufs=1))
+        stream = stack.enter_context(tc.tile_pool(name="stream", bufs=3))
+        psum = stack.enter_context(tc.psum_pool(name="psum", bufs=8))
+        stack.enter_context(tc.manual_schedule())
+
+        rows = const.tile([P, BANK], BF16)
+        nc.vector.memset(rows[:], 0.0)
+        warm = const.tile([P, 1], F32)
+        nc.vector.memset(warm[:], 0.0)
+        minus_half = const.tile([P, 1], F32)
+        nc.vector.memset(minus_half[:], -0.5)
+        ident_f32 = const.tile([P, P], F32)
+        make_identity(nc, ident_f32[:])
+        ident_bf = const.tile([P, P], BF16)
+        make_identity(nc, ident_bf[:])
+        nc.sync.dma_start(out=rows[0:2, :], in_=out_proj_b.rearrange("(r n) -> r n", n=BANK))
+        nc.sync.dma_start(out=rows[2:4, :], in_=w_norm2.rearrange("(r n) -> r n", n=BANK))
+        nc.sync.dma_start(out=rows[4:8, :], in_=b1.rearrange("(r n) -> r n", n=BANK))
+        nc.scalar.activation(out=warm[:], in_=warm[:], func=ACT.Gelu)
+
+        x_view = x.rearrange("(p j) b d -> p j b d", j=POS)
+        out0_view = out_0.rearrange("(p j) b d -> p j b d", j=POS)
+        out1_view = out_1.rearrange("(p j) b f -> p j b f", j=POS)
+        c_raw = {}
+        x_raw = {}
+        wo_raw = {}
+        w1_raw = {}
+
+        def load_heads(b):
+            for h in range(HEADS):
+                c_raw[b, h] = raw.tile([P, POS * HEAD_DIM], BF16, name="c_raw_%d_%d" % (b, h))
+                nc.sync.dma_start(out=c_raw[b, h][:], in_=h_attn[b, h].rearrange("(p j) d -> p (j d)", j=POS))
+
+        def load_x(b):
+            x_raw[b] = raw.tile([P, POS * DIM], BF16, name="x_raw_%d" % b)
+            nc.sync.dma_start(out=x_raw[b][:].rearrange("p (j d) -> p j d", j=POS), in_=x_view[:, :, b, :])
+
+        def load_weight(store, name, w, n):
+            store[n] = raw.tile([P, PACK * DIM], BF16, name="%s_%d" % (name, n))
+            nc.sync.dma_start(
+                out=store[n][:].rearrange("p (a k) -> p a k", a=PACK),
+                in_=w[n * BANK : (n + 1) * BANK, :].rearrange("(a p) k -> p a k", p=P),
+            )
+
+        load_heads(0)
+        load_x(0)
+        load_weight(wo_raw, "wo_raw", out_proj_w, 0)
+        load_weight(wo_raw, "wo_raw", out_proj_w, 1)
+        load_weight(w1_raw, "w1_raw", W1, 0)
+        load_heads(1)
+        load_x(1)
+        load_weight(w1_raw, "w1_raw", W1, 1)
+        load_weight(w1_raw, "w1_raw", W1, 2)
+        load_weight(w1_raw, "w1_raw", W1, 3)
+
+        c_codes = keep.tile([P, TOKEN_TILES, PASSES, P], U32, align_bytes=64)
+        c_scales = keep.tile([P, TOKEN_TILES, PASSES, P], U8, align_bytes=64)
+        m_codes = keep.tile([P, TOKEN_TILES, PASSES, P], U32, align_bytes=64)
+        m_scales = keep.tile([P, TOKEN_TILES, PASSES, P], U8, align_bytes=64)
+        wo_codes = keep.tile([P, PASSES, DIM], U32, align_bytes=64)
+        wo_scales = keep.tile([P, PASSES, DIM], U8, align_bytes=64)
+        w1_codes = keep.tile([P, PASSES, FF], U32, align_bytes=64)
+        w1_scales = keep.tile([P, PASSES, FF], U8, align_bytes=64)
+
+        spread = const.tile([P, 8, BANK], BF16)
+        bo_b = spread[:, 0:2, :].rearrange("p r n -> p (r n)")
+        w2_b = spread[:, 2:4, :].rearrange("p r n -> p (r n)")
+        b1_b = spread[:, 4:8, :].rearrange("p r n -> p (r n)")
+        mean_sq = const.tile([P, TOKEN_TILES], F32)
+        ms_eps = const.tile([P, TOKEN_TILES], F32)
+        rstd = const.tile([P, TOKEN_TILES], F32)
+
+        def spread_row(r):
+            bank = psum.tile([P, BANK], F32, tag="bank")
+            nc.tensor.matmul(
+                out=bank[:], lhsT=ident_bf[:, r : r + 1].to_broadcast([P, P]), rhs=rows[:], start=True, stop=True
+            )
+            nc.scalar.copy(out=spread[:, r, :], in_=bank[:])
+
+        def token_unit(first):
+            b, j = divmod(first, POS)
+            blocks = [
+                c_raw[b, g][:].bitcast(F32)[:, (j + i) * PAIRS : (j + i + 1) * PAIRS]
+                for i in range(2)
+                for g in range(PASSES)
+            ]
+            return (
+                blocks,
+                c_codes[:, first : first + 2, :, :].rearrange("p t g r -> p (t g r)"),
+                c_scales[:, first : first + 2, :, :].rearrange("p t g r -> p (t g r)"),
+            )
+
+        def weight_unit(w_raw, codes, scales, n, g):
+            words = w_raw[n][:].bitcast(F32)
+            blocks = [
+                words[:, (a * PASSES + g) * PAIRS : (a * PASSES + g + 1) * PAIRS] for a in range(PACK)
+            ]
+            cols = slice(n * BANK, (n + 1) * BANK)
+            return (blocks, codes[:, g, cols], scales[:, g, cols])
+
+        first_units = [token_unit(0), token_unit(2)]
+        first_units += [weight_unit(wo_raw, wo_codes, wo_scales, n, g) for n in range(2) for g in range(PASSES)]
+        units = [weight_unit(w1_raw, w1_codes, w1_scales, 0, g) for g in range(PASSES)]
+        units += [token_unit(4), token_unit(6)]
+        units += [weight_unit(w1_raw, w1_codes, w1_scales, n, g) for n in (1, 2, 3) for g in range(PASSES)]
+
+        def regroup(unit):
+            blocks = unit[0]
+            grouped = stream.tile([P, PACK * BANK], BF16, align_bytes=64, bufs=2 * UNITS_PER_ROUND)
+            grouped_words = grouped[:].bitcast(F32).rearrange("p (i r u) -> p i r u", i=4, u=2)
+            for half in range(2):
+                bank = psum.tile([P, 2, 2, P], F32, tag="bank")
+                for i in range(2):
+                    for u in range(2):
+                        nc.tensor.transpose(
+                            bank[:, i, u, :], blocks[2 * half + i][:, u * P : (u + 1) * P], ident_f32[:]
+                        )
+                nc.scalar.copy(
+                    out=grouped_words[:, 2 * half : 2 * half + 2, :, :],
+                    in_=bank[:].rearrange("p i u r -> p i r u"),
+                )
+            return grouped
+
+        def quantise(unit, grouped):
+            nc.vector.quantize_mx(out=unit[1].bitcast(FP8X4), scales=unit[2], in_=grouped[:])
+
+        x1_tiles = {}
+
+        def add_bias_to_x(t):
+            b, j = divmod(t, POS)
+            x1_tiles[t] = keep.tile([P, DIM], F32, name="x1_%d" % t)
+            nc.vector.tensor_tensor(
+                out=x1_tiles[t][:], in0=x_raw[b][:, j * DIM : (j + 1) * DIM], in1=bo_b, op=ALU.add
+            )
+
+        acc1 = {}
+
+        def project(t):
+            for n in range(DIM // BANK):
+                cols = slice(n * BANK, (n + 1) * BANK)
+                acc1[t, n] = psum.tile([P, BANK], F32, tag="bank", name="acc1_%d_%d" % (t, n))
+                for g in range(PASSES):
+                    nc.tensor.matmul_mx(
+                        out=acc1[t, n][:],
+                        lhsT=c_codes[:, t, g, :].bitcast(FP8X4),
+                        lhsT_scale=c_scales[:, t, g, :],
+                        rhs=wo_codes[:, g, cols].bitcast(FP8X4),
+                        rhs_scale=wo_scales[:, g, cols],
+                        start=(g == 0),
+                        stop=(g == PASSES - 1),
+                    )
+
+        def add_residual(t):
+            b, j = divmod(t, POS)
+            x1 = x1_tiles[t]
+            for n in range(DIM // BANK):
+                cols = slice(n * BANK, (n + 1) * BANK)
+                nc.vector.tensor_tensor(out=x1[:, cols], in0=acc1[t, n][:], in1=x1[:, cols], op=ALU.add)
+            nc.sync.dma_start(out=out0_view[:, j, b, :], in_=x1[:])
+
+        def inverse_rms(t):
+            squares = stream.tile([P, DIM], BF16, bufs=2)
+            nc.scalar.activation(
+                out=squares[:],
+                in_=x1_tiles[t][:],
+                func=ACT.Square,
+                scale=1.0 / 32.0,
+                accum_out=mean_sq[:, t : t + 1],
+            )
+            nc.gpsimd.tensor_scalar(
+                out=ms_eps[:, t : t + 1], in0=mean_sq[:, t : t + 1], scalar1=EPS, scalar2=1.0, op0=ALU.add, op1=ALU.mult
+            )
+            nc.gpsimd.tensor_tensor(out=rstd[:, t : t + 1], in0=ms_eps[:, t : t + 1], in1=minus_half[:], op=ALU.pow)
+
+        m_tiles = {}
+
+        def normalise(t):
+            m_tiles[t] = stream.tile([P, 2, DIM // 2], BF16, name="m_%d" % t, tag="m")
+            x1_pairs = x1_tiles[t][:].rearrange("p (w e) -> p e w", e=2)
+            w2_pairs = w2_b.rearrange("p (w e) -> p e w", e=2)
+            for e in range(2):
+                nc.vector.scalar_tensor_tensor(
+                    out=m_tiles[t][:, e, :],
+                    in0=x1_pairs[:, e, :],
+                    scalar=rstd[:, t : t + 1],
+                    in1=w2_pairs[:, e, :],
+                    op0=ALU.mult,
+                    op1=ALU.mult,
+                )
+
+        grouped_m = {}
+
+        def regroup_m(t):
+            m = m_tiles[t]
+            mt = psum.tile([P, PASSES, PACK, P], BF16, tag="bank")
+            for g in range(PASSES):
+                for u in range(2):
+                    for e in range(2):
+                        w0 = (2 * g + u) * P
+                        nc.tensor.transpose(mt[:, g, 2 * u + e, :], m[:, e, w0 : w0 + P], ident_bf[:])
+            grouped_m[t] = stream.tile([P, PASSES * P * PACK], BF16, align_bytes=64, name="grouped_m_%d" % t, tag="grouped_m")
+            nc.scalar.copy(
+                out=grouped_m[t][:].rearrange("p (g r t) -> p g r t", g=PASSES, t=PACK),
+                in_=mt[:].rearrange("p g t r -> p g r t"),
+            )
+
+        def quantise_m(t):
+            nc.vector.quantize_mx(
+                out=m_codes[:, t, :, :].rearrange("p g r -> p (g r)").bitcast(FP8X4),
+                scales=m_scales[:, t, :, :].rearrange("p g r -> p (g r)"),
+                in_=grouped_m[t][:],
+            )
+
+        acc2 = {}
+        z_tiles = {}
+
+        def up_project(t):
+            for n in range(FF // BANK):
+                cols = slice(n * BANK, (n + 1) * BANK)
+                acc2[t, n] = psum.tile([P, BANK], F32, tag="bank", name="acc2_%d_%d" % (t, n))
+                for g in range(PASSES):
+                    nc.tensor.matmul_mx(
+                        out=acc2[t, n][:],
+                        lhsT=m_codes[:, t, g, :].bitcast(FP8X4),
+                        lhsT_scale=m_scales[:, t, g, :],
+                        rhs=w1_codes[:, g, cols].bitcast(FP8X4),
+                        rhs_scale=w1_scales[:, g, cols],
+                        start=(g == 0),
+                        stop=(g == PASSES - 1),
+                    )
+
+        def add_b1(t):
+            z_tiles[t] = stream.tile([P, FF], F32, name="z_%d" % t, tag="z")
+            for n in range(FF // BANK):
+                cols = slice(n * BANK, (n + 1) * BANK)
+                nc.vector.tensor_tensor(out=z_tiles[t][:, cols], in0=acc2[t, n][:], in1=b1_b[:, cols], op=ALU.add)
+
+        def gelu_and_store(t):
+            b, j = divmod(t, POS)
+            z = z_tiles[t]
+            for half in range(2):
+                for n in (2 * half, 2 * half + 1):
+                    cols = slice(n * BANK, (n + 1) * BANK)
+                    nc.scalar.activation(out=z[:, cols], in_=z[:, cols], func=ACT.Gelu)
+                cols = slice(half * FF // 2, (half + 1) * FF // 2)
+                nc.sync.dma_start(out=out1_view[:, j, b, cols], in_=z[:, cols])
+
+        grouped_first = {}
+        grouped_first[0] = regroup(first_units[0])
+        grouped_first[1] = regroup(first_units[1])
+        for r in range(4):
+            spread_row(r)
+        quantise(first_units[0], grouped_first[0])
+        quantise(first_units[1], grouped_first[1])
+        for i in range(4):
+            grouped_first[2 + i] = regroup(first_units[2 + i])
+            add_bias_to_x(i)
+            if i > 0:
+                quantise(first_units[1 + i], grouped_first[1 + i])
+        quantise(first_units[5], grouped_first[5])
+        project(0)
+
+        unit_rounds = (len(units) + UNITS_PER_ROUND - 1) // UNITS_PER_ROUND
+        first_up_round = unit_rounds + 1
+        grouped_tiles = {}
+        for r in range(first_up_round + TOKEN_TILES + 1):
+            q = r - first_up_round
+            if 0 <= q < TOKEN_TILES:
+                up_project(q)
+            if r < TOKEN_TILES:
+                add_residual(r)
+            if 1 <= r <= TOKEN_TILES:
+                normalise(r - 1)
+            if 1 <= q <= TOKEN_TILES:
+                gelu_and_store(q - 1)
+            if r < TOKEN_TILES:
+                inverse_rms(r)
+            if 1 <= r <= TOKEN_TILES:
+                regroup_m(r - 1)
+            if 0 <= q < TOKEN_TILES:
+                add_b1(q)
+            for u in range((r - 1) * UNITS_PER_ROUND, r * UNITS_PER_ROUND):
+                if 0 <= u < len(units):
+                    quantise(units[u], grouped_tiles[u])
+            if r + 1 < TOKEN_TILES:
+                project(r + 1)
+            for u in range(r * UNITS_PER_ROUND, (r + 1) * UNITS_PER_ROUND):
+                if u < len(units):
+                    grouped_tiles[u] = regroup(units[u])
+            if r == POS - 1:
+                for i in range(4, 8):
+                    spread_row(i)
+            if 1 <= r <= POS:
+                add_bias_to_x(r + POS - 1)
+            if 1 <= r <= TOKEN_TILES:
+                quantise_m(r - 1)

@@ -51,9 +51,6 @@ def tile_transformerblock_pb_kernel(
         make_identity(nc, ident_f32[:])
         ident_bf = const.tile([P, P], BF16)
         make_identity(nc, ident_bf[:])
-        nc.sync.dma_start(out=rows[0:2, :], in_=out_proj_b.rearrange("(r n) -> r n", n=BANK))
-        nc.sync.dma_start(out=rows[2:4, :], in_=w_norm2.rearrange("(r n) -> r n", n=BANK))
-        nc.sync.dma_start(out=rows[4:8, :], in_=b1.rearrange("(r n) -> r n", n=BANK))
         nc.scalar.activation(out=warm[:], in_=warm[:], func=ACT.Gelu)
 
         x_view = x.rearrange("(p j) b d -> p j b d", j=POS)
@@ -81,6 +78,9 @@ def tile_transformerblock_pb_kernel(
             )
 
         load_heads(0)
+        nc.sync.dma_start(out=rows[0:2, :], in_=out_proj_b.rearrange("(r n) -> r n", n=BANK))
+        nc.sync.dma_start(out=rows[2:4, :], in_=w_norm2.rearrange("(r n) -> r n", n=BANK))
+        nc.sync.dma_start(out=rows[4:8, :], in_=b1.rearrange("(r n) -> r n", n=BANK))
         load_x(0)
         load_weight(wo_raw, "wo_raw", out_proj_w, 0)
         load_weight(wo_raw, "wo_raw", out_proj_w, 1)
@@ -91,8 +91,8 @@ def tile_transformerblock_pb_kernel(
         load_weight(w1_raw, "w1_raw", W1, 2)
         load_weight(w1_raw, "w1_raw", W1, 3)
 
-        c_codes = keep.tile([P, TOKEN_TILES, PASSES, P], U32, align_bytes=64)
-        c_scales = keep.tile([P, TOKEN_TILES, PASSES, P], U8, align_bytes=64)
+        c_codes = keep.tile([P, BATCH, PASSES, POS, P], U32, align_bytes=64)
+        c_scales = keep.tile([P, BATCH, PASSES, POS, P], U8, align_bytes=64)
         m_codes = keep.tile([P, TOKEN_TILES, PASSES, P], U32, align_bytes=64)
         m_scales = keep.tile([P, TOKEN_TILES, PASSES, P], U8, align_bytes=64)
         wo_codes = keep.tile([P, PASSES, DIM], U32, align_bytes=64)
@@ -115,17 +115,13 @@ def tile_transformerblock_pb_kernel(
             )
             nc.scalar.copy(out=spread[:, r, :], in_=bank[:])
 
-        def token_unit(first):
-            b, j = divmod(first, POS)
-            blocks = [
-                c_raw[b, g][:].bitcast(F32)[:, (j + i) * PAIRS : (j + i + 1) * PAIRS]
-                for i in range(2)
-                for g in range(PASSES)
-            ]
+        def token_unit(b, g):
+            words = c_raw[b, g][:].bitcast(F32)
+            blocks = [words[:, j * PAIRS : (j + 1) * PAIRS] for j in range(POS)]
             return (
                 blocks,
-                c_codes[:, first : first + 2, :, :].rearrange("p t g r -> p (t g r)"),
-                c_scales[:, first : first + 2, :, :].rearrange("p t g r -> p (t g r)"),
+                c_codes[:, b, g, :, :].rearrange("p j r -> p (j r)"),
+                c_scales[:, b, g, :, :].rearrange("p j r -> p (j r)"),
             )
 
         def weight_unit(w_raw, codes, scales, n, g):
@@ -136,16 +132,15 @@ def tile_transformerblock_pb_kernel(
             cols = slice(n * BANK, (n + 1) * BANK)
             return (blocks, codes[:, g, cols], scales[:, g, cols])
 
-        first_units = [token_unit(0), token_unit(2)]
+        first_units = [token_unit(0, g) for g in range(PASSES)]
         first_units += [weight_unit(wo_raw, wo_codes, wo_scales, n, g) for n in range(2) for g in range(PASSES)]
         units = [weight_unit(w1_raw, w1_codes, w1_scales, 0, g) for g in range(PASSES)]
-        units += [token_unit(4), token_unit(6)]
+        units += [token_unit(1, g) for g in range(PASSES)]
         units += [weight_unit(w1_raw, w1_codes, w1_scales, n, g) for n in (1, 2, 3) for g in range(PASSES)]
 
-        def regroup(unit):
+        def transpose_unit(unit):
             blocks = unit[0]
-            grouped = stream.tile([P, PACK * BANK], BF16, align_bytes=64, bufs=2 * UNITS_PER_ROUND)
-            grouped_words = grouped[:].bitcast(F32).rearrange("p (i r u) -> p i r u", i=4, u=2)
+            banks = []
             for half in range(2):
                 bank = psum.tile([P, 2, 2, P], F32, tag="bank")
                 for i in range(2):
@@ -153,11 +148,21 @@ def tile_transformerblock_pb_kernel(
                         nc.tensor.transpose(
                             bank[:, i, u, :], blocks[2 * half + i][:, u * P : (u + 1) * P], ident_f32[:]
                         )
+                banks.append(bank)
+            return banks
+
+        def copy_out_unit(banks):
+            grouped = stream.tile([P, PACK * BANK], BF16, align_bytes=64, bufs=2 * UNITS_PER_ROUND)
+            grouped_words = grouped[:].bitcast(F32).rearrange("p (i r u) -> p i r u", i=4, u=2)
+            for half in range(2):
                 nc.scalar.copy(
                     out=grouped_words[:, 2 * half : 2 * half + 2, :, :],
-                    in_=bank[:].rearrange("p i u r -> p i r u"),
+                    in_=banks[half][:].rearrange("p i u r -> p i r u"),
                 )
             return grouped
+
+        def regroup(unit):
+            return copy_out_unit(transpose_unit(unit))
 
         def quantise(unit, grouped):
             nc.vector.quantize_mx(out=unit[1].bitcast(FP8X4), scales=unit[2], in_=grouped[:])
@@ -174,14 +179,15 @@ def tile_transformerblock_pb_kernel(
         acc1 = {}
 
         def project(t):
+            b, j = divmod(t, POS)
             for n in range(DIM // BANK):
                 cols = slice(n * BANK, (n + 1) * BANK)
                 acc1[t, n] = psum.tile([P, BANK], F32, tag="bank", name="acc1_%d_%d" % (t, n))
                 for g in range(PASSES):
                     nc.tensor.matmul_mx(
                         out=acc1[t, n][:],
-                        lhsT=c_codes[:, t, g, :].bitcast(FP8X4),
-                        lhsT_scale=c_scales[:, t, g, :],
+                        lhsT=c_codes[:, b, g, j, :].bitcast(FP8X4),
+                        lhsT_scale=c_scales[:, b, g, j, :],
                         rhs=wo_codes[:, g, cols].bitcast(FP8X4),
                         rhs_scale=wo_scales[:, g, cols],
                         start=(g == 0),
@@ -226,20 +232,23 @@ def tile_transformerblock_pb_kernel(
                     op1=ALU.mult,
                 )
 
+        mt_banks = {}
         grouped_m = {}
 
-        def regroup_m(t):
+        def transpose_m(t):
             m = m_tiles[t]
-            mt = psum.tile([P, PASSES, PACK, P], BF16, tag="bank")
+            mt_banks[t] = psum.tile([P, PASSES, PACK, P], BF16, tag="bank", name="mt_%d" % t)
             for g in range(PASSES):
                 for u in range(2):
                     for e in range(2):
                         w0 = (2 * g + u) * P
-                        nc.tensor.transpose(mt[:, g, 2 * u + e, :], m[:, e, w0 : w0 + P], ident_bf[:])
+                        nc.tensor.transpose(mt_banks[t][:, g, 2 * u + e, :], m[:, e, w0 : w0 + P], ident_bf[:])
+
+        def copy_out_m(t):
             grouped_m[t] = stream.tile([P, PASSES * P * PACK], BF16, align_bytes=64, name="grouped_m_%d" % t, tag="grouped_m")
             nc.scalar.copy(
                 out=grouped_m[t][:].rearrange("p (g r t) -> p g r t", g=PASSES, t=PACK),
-                in_=mt[:].rearrange("p g t r -> p g r t"),
+                in_=mt_banks[t][:].rearrange("p g t r -> p g r t"),
             )
 
         def quantise_m(t):
@@ -273,15 +282,14 @@ def tile_transformerblock_pb_kernel(
                 cols = slice(n * BANK, (n + 1) * BANK)
                 nc.vector.tensor_tensor(out=z_tiles[t][:, cols], in0=acc2[t, n][:], in1=b1_b[:, cols], op=ALU.add)
 
-        def gelu_and_store(t):
+        def gelu_and_store(t, half):
             b, j = divmod(t, POS)
             z = z_tiles[t]
-            for half in range(2):
-                for n in (2 * half, 2 * half + 1):
-                    cols = slice(n * BANK, (n + 1) * BANK)
-                    nc.scalar.activation(out=z[:, cols], in_=z[:, cols], func=ACT.Gelu)
-                cols = slice(half * FF // 2, (half + 1) * FF // 2)
-                nc.sync.dma_start(out=out1_view[:, j, b, cols], in_=z[:, cols])
+            for n in (2 * half, 2 * half + 1):
+                cols = slice(n * BANK, (n + 1) * BANK)
+                nc.scalar.activation(out=z[:, cols], in_=z[:, cols], func=ACT.Gelu)
+            cols = slice(half * FF // 2, (half + 1) * FF // 2)
+            nc.sync.dma_start(out=out1_view[:, j, b, cols], in_=z[:, cols])
 
         grouped_first = {}
         grouped_first[0] = regroup(first_units[0])
@@ -303,32 +311,40 @@ def tile_transformerblock_pb_kernel(
         grouped_tiles = {}
         for r in range(first_up_round + TOKEN_TILES + 1):
             q = r - first_up_round
+            now = [u for u in range(r * UNITS_PER_ROUND, (r + 1) * UNITS_PER_ROUND) if u < len(units)]
+            before = [u for u in range((r - 1) * UNITS_PER_ROUND, r * UNITS_PER_ROUND) if 0 <= u < len(units)]
             if 0 <= q < TOKEN_TILES:
                 up_project(q)
+            unit_banks = {}
+            for u in now:
+                unit_banks[u] = transpose_unit(units[u])
             if r < TOKEN_TILES:
                 add_residual(r)
             if 1 <= r <= TOKEN_TILES:
                 normalise(r - 1)
+            if 2 <= r <= TOKEN_TILES + 1:
+                copy_out_m(r - 2)
+                quantise_m(r - 2)
             if 1 <= q <= TOKEN_TILES:
-                gelu_and_store(q - 1)
+                gelu_and_store(q - 1, 0)
+            for u in now[:1]:
+                grouped_tiles[u] = copy_out_unit(unit_banks[u])
             if r < TOKEN_TILES:
                 inverse_rms(r)
-            if 1 <= r <= TOKEN_TILES:
-                regroup_m(r - 1)
+            if 1 <= q <= TOKEN_TILES:
+                gelu_and_store(q - 1, 1)
+            for u in now[1:]:
+                grouped_tiles[u] = copy_out_unit(unit_banks[u])
             if 0 <= q < TOKEN_TILES:
                 add_b1(q)
-            for u in range((r - 1) * UNITS_PER_ROUND, r * UNITS_PER_ROUND):
-                if 0 <= u < len(units):
-                    quantise(units[u], grouped_tiles[u])
+            for u in before:
+                quantise(units[u], grouped_tiles[u])
             if r + 1 < TOKEN_TILES:
                 project(r + 1)
-            for u in range(r * UNITS_PER_ROUND, (r + 1) * UNITS_PER_ROUND):
-                if u < len(units):
-                    grouped_tiles[u] = regroup(units[u])
+            if 1 <= r <= TOKEN_TILES:
+                transpose_m(r - 1)
             if r == POS - 1:
                 for i in range(4, 8):
                     spread_row(i)
             if 1 <= r <= POS:
                 add_bias_to_x(r + POS - 1)
-            if 1 <= r <= TOKEN_TILES:
-                quantise_m(r - 1)

@@ -39,7 +39,6 @@ def tile_transformerblock_pb_kernel(
         keep = stack.enter_context(tc.tile_pool(name="keep", bufs=1))
         stream = stack.enter_context(tc.tile_pool(name="stream", bufs=3))
         psum = stack.enter_context(tc.psum_pool(name="psum", bufs=8))
-        stack.enter_context(tc.manual_schedule())
 
         rows = const.tile([P, BANK], BF16)
         nc.vector.memset(rows[:], 0.0)

@@ -19,14 +19,14 @@ SEQ, BATCH, DIM, HEADS, FF = 512, 2, 1024, 2, 2048
 HEAD_DIM = DIM // HEADS
 PASSES = DIM // K_PASS
 POS = SEQ // P
-TOKEN_TILES = BATCH * POS
+TILES = BATCH * POS
 PAIRS = K_PASS // 2
+HALVES = PAIRS // P
 EPS = 1e-8
+BO_ROWS, W2_ROWS, B1_ROWS = DIM // BANK, DIM // BANK, FF // BANK
+UNITS_PER_ROUND = 2
 
 FLOPS = 2 * SEQ * BATCH * DIM * (DIM + FF)
-
-
-UNITS_PER_ROUND = 2
 
 
 def tile_transformerblock_pb_kernel(
@@ -39,18 +39,19 @@ def tile_transformerblock_pb_kernel(
         keep = stack.enter_context(tc.tile_pool(name="keep", bufs=1))
         stream = stack.enter_context(tc.tile_pool(name="stream", bufs=3))
         psum = stack.enter_context(tc.psum_pool(name="psum", bufs=8))
+        stack.enter_context(tc.manual_schedule())
 
-        rows = const.tile([P, BANK], BF16)
-        nc.vector.memset(rows[:], 0.0)
-        warm = const.tile([P, 1], F32)
-        nc.vector.memset(warm[:], 0.0)
+        vector_rows = const.tile([P, BANK], BF16)
+        nc.vector.memset(vector_rows[:], 0.0)
+        table_warmer = const.tile([P, 1], F32)
+        nc.vector.memset(table_warmer[:], 0.0)
         minus_half = const.tile([P, 1], F32)
         nc.vector.memset(minus_half[:], -0.5)
         ident_f32 = const.tile([P, P], F32)
         make_identity(nc, ident_f32[:])
-        ident_bf = const.tile([P, P], BF16)
-        make_identity(nc, ident_bf[:])
-        nc.scalar.activation(out=warm[:], in_=warm[:], func=ACT.Gelu)
+        ident_bf16 = const.tile([P, P], BF16)
+        make_identity(nc, ident_bf16[:])
+        nc.scalar.activation(out=table_warmer[:], in_=table_warmer[:], func=ACT.Gelu)
 
         x_view = x.rearrange("(p j) b d -> p j b d", j=POS)
         out0_view = out_0.rearrange("(p j) b d -> p j b d", j=POS)
@@ -61,25 +62,32 @@ def tile_transformerblock_pb_kernel(
         w1_raw = {}
 
         def load_heads(b):
-            for h in range(HEADS):
-                c_raw[b, h] = raw.tile([P, POS * HEAD_DIM], BF16, name="c_raw_%d_%d" % (b, h))
-                nc.sync.dma_start(out=c_raw[b, h][:], in_=h_attn[b, h].rearrange("(p j) d -> p (j d)", j=POS))
+            for head in range(HEADS):
+                c_raw[b, head] = raw.tile([P, POS * HEAD_DIM], BF16, name="c_raw_%d_%d" % (b, head))
+                nc.sync.dma_start(
+                    out=c_raw[b, head][:], in_=h_attn[b, head].rearrange("(p j) d -> p (j d)", j=POS)
+                )
 
         def load_x(b):
             x_raw[b] = raw.tile([P, POS * DIM], BF16, name="x_raw_%d" % b)
             nc.sync.dma_start(out=x_raw[b][:].rearrange("p (j d) -> p j d", j=POS), in_=x_view[:, :, b, :])
 
-        def load_weight(store, name, w, n):
-            store[n] = raw.tile([P, PACK * DIM], BF16, name="%s_%d" % (name, n))
+        def load_vector(first_row, n_rows, vector):
             nc.sync.dma_start(
-                out=store[n][:].rearrange("p (a k) -> p a k", a=PACK),
-                in_=w[n * BANK : (n + 1) * BANK, :].rearrange("(a p) k -> p a k", p=P),
+                out=vector_rows[first_row : first_row + n_rows, :], in_=vector.rearrange("(r n) -> r n", n=BANK)
+            )
+
+        def load_weight(store, name, weight, chunk):
+            store[chunk] = raw.tile([P, PACK * DIM], BF16, name="%s_%d" % (name, chunk))
+            nc.sync.dma_start(
+                out=store[chunk][:].rearrange("p (a k) -> p a k", a=PACK),
+                in_=weight[chunk * BANK : (chunk + 1) * BANK, :].rearrange("(a p) k -> p a k", p=P),
             )
 
         load_heads(0)
-        nc.sync.dma_start(out=rows[0:2, :], in_=out_proj_b.rearrange("(r n) -> r n", n=BANK))
-        nc.sync.dma_start(out=rows[2:4, :], in_=w_norm2.rearrange("(r n) -> r n", n=BANK))
-        nc.sync.dma_start(out=rows[4:8, :], in_=b1.rearrange("(r n) -> r n", n=BANK))
+        load_vector(0, BO_ROWS, out_proj_b)
+        load_vector(BO_ROWS, W2_ROWS, w_norm2)
+        load_vector(BO_ROWS + W2_ROWS, B1_ROWS, b1)
         load_x(0)
         load_weight(wo_raw, "wo_raw", out_proj_w, 0)
         load_weight(wo_raw, "wo_raw", out_proj_w, 1)
@@ -90,60 +98,55 @@ def tile_transformerblock_pb_kernel(
         load_weight(w1_raw, "w1_raw", W1, 2)
         load_weight(w1_raw, "w1_raw", W1, 3)
 
-        c_codes = keep.tile([P, BATCH, PASSES, POS, P], U32, align_bytes=64)
+        c_words = keep.tile([P, BATCH, PASSES, POS, P], U32, align_bytes=64)
         c_scales = keep.tile([P, BATCH, PASSES, POS, P], U8, align_bytes=64)
-        m_codes = keep.tile([P, TOKEN_TILES, PASSES, P], U32, align_bytes=64)
-        m_scales = keep.tile([P, TOKEN_TILES, PASSES, P], U8, align_bytes=64)
-        wo_codes = keep.tile([P, PASSES, DIM], U32, align_bytes=64)
+        m_words = keep.tile([P, TILES, PASSES, P], U32, align_bytes=64)
+        m_scales = keep.tile([P, TILES, PASSES, P], U8, align_bytes=64)
+        wo_words = keep.tile([P, PASSES, DIM], U32, align_bytes=64)
         wo_scales = keep.tile([P, PASSES, DIM], U8, align_bytes=64)
-        w1_codes = keep.tile([P, PASSES, FF], U32, align_bytes=64)
+        w1_words = keep.tile([P, PASSES, FF], U32, align_bytes=64)
         w1_scales = keep.tile([P, PASSES, FF], U8, align_bytes=64)
 
-        spread = const.tile([P, 8, BANK], BF16)
-        bo_b = spread[:, 0:2, :].rearrange("p r n -> p (r n)")
-        w2_b = spread[:, 2:4, :].rearrange("p r n -> p (r n)")
-        b1_b = spread[:, 4:8, :].rearrange("p r n -> p (r n)")
-        mean_sq = const.tile([P, TOKEN_TILES], F32)
-        ms_eps = const.tile([P, TOKEN_TILES], F32)
-        rstd = const.tile([P, TOKEN_TILES], F32)
+        spread = const.tile([P, BO_ROWS + W2_ROWS + B1_ROWS, BANK], BF16)
+        bo_all = spread[:, 0:BO_ROWS, :].rearrange("p r n -> p (r n)")
+        w2_all = spread[:, BO_ROWS : BO_ROWS + W2_ROWS, :].rearrange("p r n -> p (r n)")
+        b1_all = spread[:, BO_ROWS + W2_ROWS :, :].rearrange("p r n -> p (r n)")
 
-        def spread_row(r):
+        def spread_row(row):
             bank = psum.tile([P, BANK], F32, tag="bank")
             nc.tensor.matmul(
-                out=bank[:], lhsT=ident_bf[:, r : r + 1].to_broadcast([P, P]), rhs=rows[:], start=True, stop=True
+                out=bank[:],
+                lhsT=ident_bf16[:, row : row + 1].to_broadcast([P, P]),
+                rhs=vector_rows[:],
+                start=True,
+                stop=True,
             )
-            nc.scalar.copy(out=spread[:, r, :], in_=bank[:])
+            nc.scalar.copy(out=spread[:, row, :], in_=bank[:])
 
         def token_unit(b, g):
             words = c_raw[b, g][:].bitcast(F32)
-            blocks = [words[:, j * PAIRS : (j + 1) * PAIRS] for j in range(POS)]
             return (
-                blocks,
-                c_codes[:, b, g, :, :].rearrange("p j r -> p (j r)"),
+                [words[:, j * PAIRS : (j + 1) * PAIRS] for j in range(POS)],
+                c_words[:, b, g, :, :].rearrange("p j r -> p (j r)"),
                 c_scales[:, b, g, :, :].rearrange("p j r -> p (j r)"),
             )
 
-        def weight_unit(w_raw, codes, scales, n, g):
-            words = w_raw[n][:].bitcast(F32)
-            blocks = [
-                words[:, (a * PASSES + g) * PAIRS : (a * PASSES + g + 1) * PAIRS] for a in range(PACK)
-            ]
-            cols = slice(n * BANK, (n + 1) * BANK)
-            return (blocks, codes[:, g, cols], scales[:, g, cols])
-
-        first_units = [token_unit(0, g) for g in range(PASSES)]
-        first_units += [weight_unit(wo_raw, wo_codes, wo_scales, n, g) for n in range(2) for g in range(PASSES)]
-        units = [weight_unit(w1_raw, w1_codes, w1_scales, 0, g) for g in range(PASSES)]
-        units += [token_unit(1, g) for g in range(PASSES)]
-        units += [weight_unit(w1_raw, w1_codes, w1_scales, n, g) for n in (1, 2, 3) for g in range(PASSES)]
+        def weight_unit(w_raw, w_words, w_scales, chunk, g):
+            words = w_raw[chunk][:].bitcast(F32)
+            cols = slice(chunk * BANK, (chunk + 1) * BANK)
+            return (
+                [words[:, (a * PASSES + g) * PAIRS : (a * PASSES + g + 1) * PAIRS] for a in range(PACK)],
+                w_words[:, g, cols],
+                w_scales[:, g, cols],
+            )
 
         def transpose_unit(unit):
             blocks = unit[0]
             banks = []
             for half in range(2):
-                bank = psum.tile([P, 2, 2, P], F32, tag="bank")
+                bank = psum.tile([P, 2, HALVES, P], F32, tag="bank")
                 for i in range(2):
-                    for u in range(2):
+                    for u in range(HALVES):
                         nc.tensor.transpose(
                             bank[:, i, u, :], blocks[2 * half + i][:, u * P : (u + 1) * P], ident_f32[:]
                         )
@@ -152,7 +155,7 @@ def tile_transformerblock_pb_kernel(
 
         def copy_out_unit(banks):
             grouped = stream.tile([P, PACK * BANK], BF16, align_bytes=64, bufs=2 * UNITS_PER_ROUND)
-            grouped_words = grouped[:].bitcast(F32).rearrange("p (i r u) -> p i r u", i=4, u=2)
+            grouped_words = grouped[:].bitcast(F32).rearrange("p (i r u) -> p i r u", i=PACK, u=HALVES)
             for half in range(2):
                 nc.scalar.copy(
                     out=grouped_words[:, 2 * half : 2 * half + 2, :, :],
@@ -160,190 +163,198 @@ def tile_transformerblock_pb_kernel(
                 )
             return grouped
 
-        def regroup(unit):
-            return copy_out_unit(transpose_unit(unit))
-
-        def quantise(unit, grouped):
+        def quantise_unit(unit, grouped):
             nc.vector.quantize_mx(out=unit[1].bitcast(FP8X4), scales=unit[2], in_=grouped[:])
 
         x1_tiles = {}
 
-        def add_bias_to_x(t):
-            b, j = divmod(t, POS)
-            x1_tiles[t] = keep.tile([P, DIM], F32, name="x1_%d" % t)
+        def add_bias_to_x(tile):
+            b, j = divmod(tile, POS)
+            x1_tiles[tile] = keep.tile([P, DIM], F32, name="x1_%d" % tile)
             nc.vector.tensor_tensor(
-                out=x1_tiles[t][:], in0=x_raw[b][:, j * DIM : (j + 1) * DIM], in1=bo_b, op=ALU.add
+                out=x1_tiles[tile][:], in0=x_raw[b][:, j * DIM : (j + 1) * DIM], in1=bo_all, op=ALU.add
             )
 
-        acc1 = {}
+        attn_banks = {}
 
-        def project(t):
-            b, j = divmod(t, POS)
+        def project(tile):
+            b, j = divmod(tile, POS)
             for n in range(DIM // BANK):
                 cols = slice(n * BANK, (n + 1) * BANK)
-                acc1[t, n] = psum.tile([P, BANK], F32, tag="bank", name="acc1_%d_%d" % (t, n))
+                attn_banks[tile, n] = psum.tile([P, BANK], F32, tag="bank", name="attn_%d_%d" % (tile, n))
                 for g in range(PASSES):
                     nc.tensor.matmul_mx(
-                        out=acc1[t, n][:],
-                        lhsT=c_codes[:, b, g, j, :].bitcast(FP8X4),
+                        out=attn_banks[tile, n][:],
+                        lhsT=c_words[:, b, g, j, :].bitcast(FP8X4),
                         lhsT_scale=c_scales[:, b, g, j, :],
-                        rhs=wo_codes[:, g, cols].bitcast(FP8X4),
+                        rhs=wo_words[:, g, cols].bitcast(FP8X4),
                         rhs_scale=wo_scales[:, g, cols],
                         start=(g == 0),
                         stop=(g == PASSES - 1),
                     )
 
-        def add_residual(t):
-            b, j = divmod(t, POS)
-            x1 = x1_tiles[t]
+        def add_residual(tile):
+            b, j = divmod(tile, POS)
+            x1 = x1_tiles[tile]
             for n in range(DIM // BANK):
                 cols = slice(n * BANK, (n + 1) * BANK)
-                nc.vector.tensor_tensor(out=x1[:, cols], in0=acc1[t, n][:], in1=x1[:, cols], op=ALU.add)
+                nc.vector.tensor_tensor(out=x1[:, cols], in0=attn_banks[tile, n][:], in1=x1[:, cols], op=ALU.add)
             nc.sync.dma_start(out=out0_view[:, j, b, :], in_=x1[:])
 
-        def inverse_rms(t):
+        mean_sq = const.tile([P, TILES], F32)
+        mean_sq_eps = const.tile([P, TILES], F32)
+        inv_rms = const.tile([P, TILES], F32)
+
+        def inverse_rms(tile):
+            col = slice(tile, tile + 1)
             squares = stream.tile([P, DIM], BF16, bufs=2)
             nc.scalar.activation(
-                out=squares[:],
-                in_=x1_tiles[t][:],
-                func=ACT.Square,
-                scale=1.0 / 32.0,
-                accum_out=mean_sq[:, t : t + 1],
+                out=squares[:], in_=x1_tiles[tile][:], func=ACT.Square, scale=DIM**-0.5, accum_out=mean_sq[:, col]
             )
             nc.gpsimd.tensor_scalar(
-                out=ms_eps[:, t : t + 1], in0=mean_sq[:, t : t + 1], scalar1=EPS, scalar2=1.0, op0=ALU.add, op1=ALU.mult
+                out=mean_sq_eps[:, col], in0=mean_sq[:, col], scalar1=EPS, scalar2=1.0, op0=ALU.add, op1=ALU.mult
             )
-            nc.gpsimd.tensor_tensor(out=rstd[:, t : t + 1], in0=ms_eps[:, t : t + 1], in1=minus_half[:], op=ALU.pow)
+            nc.gpsimd.tensor_tensor(out=inv_rms[:, col], in0=mean_sq_eps[:, col], in1=minus_half[:], op=ALU.pow)
 
         m_tiles = {}
 
-        def normalise(t):
-            m_tiles[t] = stream.tile([P, 2, DIM // 2], BF16, name="m_%d" % t, tag="m")
-            x1_pairs = x1_tiles[t][:].rearrange("p (w e) -> p e w", e=2)
-            w2_pairs = w2_b.rearrange("p (w e) -> p e w", e=2)
+        def normalise(tile):
+            m_tiles[tile] = stream.tile([P, 2, DIM // 2], BF16, name="m_%d" % tile, tag="m")
+            x1_planes = x1_tiles[tile][:].rearrange("p (w e) -> p e w", e=2)
+            w2_planes = w2_all.rearrange("p (w e) -> p e w", e=2)
             for e in range(2):
                 nc.vector.scalar_tensor_tensor(
-                    out=m_tiles[t][:, e, :],
-                    in0=x1_pairs[:, e, :],
-                    scalar=rstd[:, t : t + 1],
-                    in1=w2_pairs[:, e, :],
+                    out=m_tiles[tile][:, e, :],
+                    in0=x1_planes[:, e, :],
+                    scalar=inv_rms[:, tile : tile + 1],
+                    in1=w2_planes[:, e, :],
                     op0=ALU.mult,
                     op1=ALU.mult,
                 )
 
-        mt_banks = {}
+        m_banks = {}
+
+        def transpose_m(tile):
+            m_banks[tile] = psum.tile([P, PASSES, PACK, P], BF16, tag="bank", name="m_bank_%d" % tile)
+            for g in range(PASSES):
+                for u in range(HALVES):
+                    for e in range(2):
+                        first = (HALVES * g + u) * P
+                        nc.tensor.transpose(
+                            m_banks[tile][:, g, 2 * u + e, :], m_tiles[tile][:, e, first : first + P], ident_bf16[:]
+                        )
+
         grouped_m = {}
 
-        def transpose_m(t):
-            m = m_tiles[t]
-            mt_banks[t] = psum.tile([P, PASSES, PACK, P], BF16, tag="bank", name="mt_%d" % t)
-            for g in range(PASSES):
-                for u in range(2):
-                    for e in range(2):
-                        w0 = (2 * g + u) * P
-                        nc.tensor.transpose(mt_banks[t][:, g, 2 * u + e, :], m[:, e, w0 : w0 + P], ident_bf[:])
-
-        def copy_out_m(t):
-            grouped_m[t] = stream.tile([P, PASSES * P * PACK], BF16, align_bytes=64, name="grouped_m_%d" % t, tag="grouped_m")
+        def copy_out_m(tile):
+            grouped_m[tile] = stream.tile(
+                [P, PASSES * P * PACK], BF16, align_bytes=64, name="grouped_m_%d" % tile, tag="grouped_m"
+            )
             nc.scalar.copy(
-                out=grouped_m[t][:].rearrange("p (g r t) -> p g r t", g=PASSES, t=PACK),
-                in_=mt_banks[t][:].rearrange("p g t r -> p g r t"),
+                out=grouped_m[tile][:].rearrange("p (g r v) -> p g r v", g=PASSES, v=PACK),
+                in_=m_banks[tile][:].rearrange("p g v r -> p g r v"),
             )
 
-        def quantise_m(t):
+        def quantise_m(tile):
             nc.vector.quantize_mx(
-                out=m_codes[:, t, :, :].rearrange("p g r -> p (g r)").bitcast(FP8X4),
-                scales=m_scales[:, t, :, :].rearrange("p g r -> p (g r)"),
-                in_=grouped_m[t][:],
+                out=m_words[:, tile, :, :].rearrange("p g r -> p (g r)").bitcast(FP8X4),
+                scales=m_scales[:, tile, :, :].rearrange("p g r -> p (g r)"),
+                in_=grouped_m[tile][:],
             )
 
-        acc2 = {}
-        z_tiles = {}
+        up_banks = {}
 
-        def up_project(t):
+        def up_project(tile):
             for n in range(FF // BANK):
                 cols = slice(n * BANK, (n + 1) * BANK)
-                acc2[t, n] = psum.tile([P, BANK], F32, tag="bank", name="acc2_%d_%d" % (t, n))
+                up_banks[tile, n] = psum.tile([P, BANK], F32, tag="bank", name="up_%d_%d" % (tile, n))
                 for g in range(PASSES):
                     nc.tensor.matmul_mx(
-                        out=acc2[t, n][:],
-                        lhsT=m_codes[:, t, g, :].bitcast(FP8X4),
-                        lhsT_scale=m_scales[:, t, g, :],
-                        rhs=w1_codes[:, g, cols].bitcast(FP8X4),
+                        out=up_banks[tile, n][:],
+                        lhsT=m_words[:, tile, g, :].bitcast(FP8X4),
+                        lhsT_scale=m_scales[:, tile, g, :],
+                        rhs=w1_words[:, g, cols].bitcast(FP8X4),
                         rhs_scale=w1_scales[:, g, cols],
                         start=(g == 0),
                         stop=(g == PASSES - 1),
                     )
 
-        def add_b1(t):
-            z_tiles[t] = stream.tile([P, FF], F32, name="z_%d" % t, tag="z")
+        g_tiles = {}
+
+        def add_b1(tile):
+            g_tiles[tile] = stream.tile([P, FF], F32, name="g_%d" % tile, tag="g")
             for n in range(FF // BANK):
                 cols = slice(n * BANK, (n + 1) * BANK)
-                nc.vector.tensor_tensor(out=z_tiles[t][:, cols], in0=acc2[t, n][:], in1=b1_b[:, cols], op=ALU.add)
+                nc.vector.tensor_tensor(
+                    out=g_tiles[tile][:, cols], in0=up_banks[tile, n][:], in1=b1_all[:, cols], op=ALU.add
+                )
 
-        def gelu_and_store(t, half):
-            b, j = divmod(t, POS)
-            z = z_tiles[t]
+        def gelu_and_store(tile, half):
+            b, j = divmod(tile, POS)
             for n in (2 * half, 2 * half + 1):
                 cols = slice(n * BANK, (n + 1) * BANK)
-                nc.scalar.activation(out=z[:, cols], in_=z[:, cols], func=ACT.Gelu)
+                nc.scalar.activation(out=g_tiles[tile][:, cols], in_=g_tiles[tile][:, cols], func=ACT.Gelu)
             cols = slice(half * FF // 2, (half + 1) * FF // 2)
-            nc.sync.dma_start(out=out1_view[:, j, b, cols], in_=z[:, cols])
+            nc.sync.dma_start(out=out1_view[:, j, b, cols], in_=g_tiles[tile][:, cols])
 
-        grouped_first = {}
-        grouped_first[0] = regroup(first_units[0])
-        grouped_first[1] = regroup(first_units[1])
-        for r in range(4):
-            spread_row(r)
-        quantise(first_units[0], grouped_first[0])
-        quantise(first_units[1], grouped_first[1])
-        for i in range(4):
-            grouped_first[2 + i] = regroup(first_units[2 + i])
+        token_units = [token_unit(0, g) for g in range(PASSES)]
+        token_grouped = [copy_out_unit(transpose_unit(unit)) for unit in token_units]
+        for row in range(BO_ROWS + W2_ROWS):
+            spread_row(row)
+        for unit, grouped in zip(token_units, token_grouped):
+            quantise_unit(unit, grouped)
+        wo_units = [weight_unit(wo_raw, wo_words, wo_scales, chunk, g) for chunk in range(2) for g in range(PASSES)]
+        wo_grouped = []
+        for i in range(len(wo_units)):
+            wo_grouped.append(copy_out_unit(transpose_unit(wo_units[i])))
             add_bias_to_x(i)
             if i > 0:
-                quantise(first_units[1 + i], grouped_first[1 + i])
-        quantise(first_units[5], grouped_first[5])
+                quantise_unit(wo_units[i - 1], wo_grouped[i - 1])
+        quantise_unit(wo_units[-1], wo_grouped[-1])
         project(0)
 
+        units = [weight_unit(w1_raw, w1_words, w1_scales, 0, g) for g in range(PASSES)]
+        units += [token_unit(1, g) for g in range(PASSES)]
+        units += [weight_unit(w1_raw, w1_words, w1_scales, chunk, g) for chunk in (1, 2, 3) for g in range(PASSES)]
         unit_rounds = (len(units) + UNITS_PER_ROUND - 1) // UNITS_PER_ROUND
         first_up_round = unit_rounds + 1
-        grouped_tiles = {}
-        for r in range(first_up_round + TOKEN_TILES + 1):
-            q = r - first_up_round
-            now = [u for u in range(r * UNITS_PER_ROUND, (r + 1) * UNITS_PER_ROUND) if u < len(units)]
-            before = [u for u in range((r - 1) * UNITS_PER_ROUND, r * UNITS_PER_ROUND) if 0 <= u < len(units)]
-            if 0 <= q < TOKEN_TILES:
-                up_project(q)
+        unit_grouped = {}
+        for rnd in range(first_up_round + TILES + 1):
+            up = rnd - first_up_round
+            now = [i for i in range(rnd * UNITS_PER_ROUND, (rnd + 1) * UNITS_PER_ROUND) if i < len(units)]
+            before = [i for i in range((rnd - 1) * UNITS_PER_ROUND, rnd * UNITS_PER_ROUND) if 0 <= i < len(units)]
+            if 0 <= up < TILES:
+                up_project(up)
             unit_banks = {}
-            for u in now:
-                unit_banks[u] = transpose_unit(units[u])
-            if r < TOKEN_TILES:
-                add_residual(r)
-            if 1 <= r <= TOKEN_TILES:
-                normalise(r - 1)
-            if 2 <= r <= TOKEN_TILES + 1:
-                copy_out_m(r - 2)
-                quantise_m(r - 2)
-            if 1 <= q <= TOKEN_TILES:
-                gelu_and_store(q - 1, 0)
-            for u in now[:1]:
-                grouped_tiles[u] = copy_out_unit(unit_banks[u])
-            if r < TOKEN_TILES:
-                inverse_rms(r)
-            if 1 <= q <= TOKEN_TILES:
-                gelu_and_store(q - 1, 1)
-            for u in now[1:]:
-                grouped_tiles[u] = copy_out_unit(unit_banks[u])
-            if 0 <= q < TOKEN_TILES:
-                add_b1(q)
-            for u in before:
-                quantise(units[u], grouped_tiles[u])
-            if r + 1 < TOKEN_TILES:
-                project(r + 1)
-            if 1 <= r <= TOKEN_TILES:
-                transpose_m(r - 1)
-            if r == POS - 1:
-                for i in range(4, 8):
-                    spread_row(i)
-            if 1 <= r <= POS:
-                add_bias_to_x(r + POS - 1)
+            for i in now:
+                unit_banks[i] = transpose_unit(units[i])
+            if rnd < TILES:
+                add_residual(rnd)
+            if 1 <= rnd <= TILES:
+                normalise(rnd - 1)
+            if 2 <= rnd <= TILES + 1:
+                copy_out_m(rnd - 2)
+                quantise_m(rnd - 2)
+            if 1 <= up <= TILES:
+                gelu_and_store(up - 1, 0)
+            for i in now[:1]:
+                unit_grouped[i] = copy_out_unit(unit_banks[i])
+            if rnd < TILES:
+                inverse_rms(rnd)
+            if 1 <= up <= TILES:
+                gelu_and_store(up - 1, 1)
+            for i in now[1:]:
+                unit_grouped[i] = copy_out_unit(unit_banks[i])
+            if 0 <= up < TILES:
+                add_b1(up)
+            for i in before:
+                quantise_unit(units[i], unit_grouped[i])
+            if rnd + 1 < TILES:
+                project(rnd + 1)
+            if 1 <= rnd <= TILES:
+                transpose_m(rnd - 1)
+            if rnd == unit_rounds - 1:
+                for row in range(BO_ROWS + W2_ROWS, BO_ROWS + W2_ROWS + B1_ROWS):
+                    spread_row(row)
+            if 1 <= rnd <= POS:
+                add_bias_to_x(rnd + POS - 1)

from contextlib import ExitStack

import concourse.mybir as mybir
from concourse.masks import make_identity

BF16 = mybir.dt.bfloat16
F32 = mybir.dt.float32
U32 = mybir.dt.uint32
U8 = mybir.dt.uint8
FP8X4 = mybir.dt.float8_e4m3fn_x4
ALU = mybir.AluOpType
ACT = mybir.ActivationFunctionType

P = 128
PACK = 4
K_PASS = P * PACK
BANK = 512
SEQ, BATCH, DIM, HEADS, FF = 512, 2, 1024, 2, 2048
HEAD_DIM = DIM // HEADS
PASSES = DIM // K_PASS
POS = SEQ // P
TILES = BATCH * POS
PAIRS = K_PASS // 2
HALVES = PAIRS // P
EPS = 1e-8
BO_ROWS, W2_ROWS, B1_ROWS = DIM // BANK, DIM // BANK, FF // BANK
UNITS_PER_ROUND = 2

FLOPS = 2 * SEQ * BATCH * DIM * (DIM + FF)


def tile_transformerblock_pb_kernel(
    tc, h_attn, x, out_proj_w, out_proj_b, w_norm2, W1, b1, out_0, out_1
):
    nc = tc.nc
    with ExitStack() as stack:
        const = stack.enter_context(tc.tile_pool(name="const", bufs=1))
        raw = stack.enter_context(tc.tile_pool(name="raw", bufs=1))
        keep = stack.enter_context(tc.tile_pool(name="keep", bufs=1))
        stream = stack.enter_context(tc.tile_pool(name="stream", bufs=3))
        psum = stack.enter_context(tc.psum_pool(name="psum", bufs=8))
        stack.enter_context(tc.manual_schedule())

        vector_rows = const.tile([P, BANK], BF16)
        nc.vector.memset(vector_rows[:], 0.0)
        table_warmer = const.tile([P, 1], F32)
        nc.vector.memset(table_warmer[:], 0.0)
        minus_half = const.tile([P, 1], F32)
        nc.vector.memset(minus_half[:], -0.5)
        ident_f32 = const.tile([P, P], F32)
        make_identity(nc, ident_f32[:])
        ident_bf16 = const.tile([P, P], BF16)
        make_identity(nc, ident_bf16[:])
        nc.scalar.activation(out=table_warmer[:], in_=table_warmer[:], func=ACT.Gelu)

        x_view = x.rearrange("(p j) b d -> p j b d", j=POS)
        out0_view = out_0.rearrange("(p j) b d -> p j b d", j=POS)
        out1_view = out_1.rearrange("(p j) b f -> p j b f", j=POS)
        c_raw = {}
        x_raw = {}
        wo_raw = {}
        w1_raw = {}

        def load_heads(b):
            for head in range(HEADS):
                c_raw[b, head] = raw.tile([P, POS * HEAD_DIM], BF16, name="c_raw_%d_%d" % (b, head))
                nc.sync.dma_start(
                    out=c_raw[b, head][:], in_=h_attn[b, head].rearrange("(p j) d -> p (j d)", j=POS)
                )

        def load_x(b):
            x_raw[b] = raw.tile([P, POS * DIM], BF16, name="x_raw_%d" % b)
            nc.sync.dma_start(out=x_raw[b][:].rearrange("p (j d) -> p j d", j=POS), in_=x_view[:, :, b, :])

        def load_vector(first_row, n_rows, vector):
            nc.sync.dma_start(
                out=vector_rows[first_row : first_row + n_rows, :], in_=vector.rearrange("(r n) -> r n", n=BANK)
            )

        def load_weight(store, name, weight, chunk):
            store[chunk] = raw.tile([P, PACK * DIM], BF16, name="%s_%d" % (name, chunk))
            nc.sync.dma_start(
                out=store[chunk][:].rearrange("p (a k) -> p a k", a=PACK),
                in_=weight[chunk * BANK : (chunk + 1) * BANK, :].rearrange("(a p) k -> p a k", p=P),
            )

        load_heads(0)
        load_vector(0, BO_ROWS, out_proj_b)
        load_vector(BO_ROWS, W2_ROWS, w_norm2)
        load_vector(BO_ROWS + W2_ROWS, B1_ROWS, b1)
        load_x(0)
        load_weight(wo_raw, "wo_raw", out_proj_w, 0)
        load_weight(wo_raw, "wo_raw", out_proj_w, 1)
        load_weight(w1_raw, "w1_raw", W1, 0)
        load_heads(1)
        load_x(1)
        load_weight(w1_raw, "w1_raw", W1, 1)
        load_weight(w1_raw, "w1_raw", W1, 2)
        load_weight(w1_raw, "w1_raw", W1, 3)

        c_words = keep.tile([P, BATCH, PASSES, POS, P], U32, align_bytes=64)
        c_scales = keep.tile([P, BATCH, PASSES, POS, P], U8, align_bytes=64)
        m_words = keep.tile([P, TILES, PASSES, P], U32, align_bytes=64)
        m_scales = keep.tile([P, TILES, PASSES, P], U8, align_bytes=64)
        wo_words = keep.tile([P, PASSES, DIM], U32, align_bytes=64)
        wo_scales = keep.tile([P, PASSES, DIM], U8, align_bytes=64)
        w1_words = keep.tile([P, PASSES, FF], U32, align_bytes=64)
        w1_scales = keep.tile([P, PASSES, FF], U8, align_bytes=64)

        spread = const.tile([P, BO_ROWS + W2_ROWS + B1_ROWS, BANK], BF16)
        bo_all = spread[:, 0:BO_ROWS, :].rearrange("p r n -> p (r n)")
        w2_all = spread[:, BO_ROWS : BO_ROWS + W2_ROWS, :].rearrange("p r n -> p (r n)")
        b1_all = spread[:, BO_ROWS + W2_ROWS :, :].rearrange("p r n -> p (r n)")

        def spread_row(row):
            bank = psum.tile([P, BANK], F32, tag="bank")
            nc.tensor.matmul(
                out=bank[:],
                lhsT=ident_bf16[:, row : row + 1].to_broadcast([P, P]),
                rhs=vector_rows[:],
                start=True,
                stop=True,
            )
            nc.scalar.copy(out=spread[:, row, :], in_=bank[:])

        def token_unit(b, g):
            words = c_raw[b, g][:].bitcast(F32)
            return (
                [words[:, j * PAIRS : (j + 1) * PAIRS] for j in range(POS)],
                c_words[:, b, g, :, :].rearrange("p j r -> p (j r)"),
                c_scales[:, b, g, :, :].rearrange("p j r -> p (j r)"),
            )

        def weight_unit(w_raw, w_words, w_scales, chunk, g):
            words = w_raw[chunk][:].bitcast(F32)
            cols = slice(chunk * BANK, (chunk + 1) * BANK)
            return (
                [words[:, (a * PASSES + g) * PAIRS : (a * PASSES + g + 1) * PAIRS] for a in range(PACK)],
                w_words[:, g, cols],
                w_scales[:, g, cols],
            )

        def transpose_unit(unit):
            blocks = unit[0]
            banks = []
            for half in range(2):
                bank = psum.tile([P, 2, HALVES, P], F32, tag="bank")
                for i in range(2):
                    for u in range(HALVES):
                        nc.tensor.transpose(
                            bank[:, i, u, :], blocks[2 * half + i][:, u * P : (u + 1) * P], ident_f32[:]
                        )
                banks.append(bank)
            return banks

        def copy_out_unit(banks):
            grouped = stream.tile([P, PACK * BANK], BF16, align_bytes=64, bufs=2 * UNITS_PER_ROUND)
            grouped_words = grouped[:].bitcast(F32).rearrange("p (i r u) -> p i r u", i=PACK, u=HALVES)
            for half in range(2):
                nc.scalar.copy(
                    out=grouped_words[:, 2 * half : 2 * half + 2, :, :],
                    in_=banks[half][:].rearrange("p i u r -> p i r u"),
                )
            return grouped

        def quantise_unit(unit, grouped):
            nc.vector.quantize_mx(out=unit[1].bitcast(FP8X4), scales=unit[2], in_=grouped[:])

        x1_tiles = {}

        def add_bias_to_x(tile):
            b, j = divmod(tile, POS)
            x1_tiles[tile] = keep.tile([P, DIM], F32, name="x1_%d" % tile)
            nc.vector.tensor_tensor(
                out=x1_tiles[tile][:], in0=x_raw[b][:, j * DIM : (j + 1) * DIM], in1=bo_all, op=ALU.add
            )

        attn_banks = {}

        def project(tile):
            b, j = divmod(tile, POS)
            for n in range(DIM // BANK):
                cols = slice(n * BANK, (n + 1) * BANK)
                attn_banks[tile, n] = psum.tile([P, BANK], F32, tag="bank", name="attn_%d_%d" % (tile, n))
                for g in range(PASSES):
                    nc.tensor.matmul_mx(
                        out=attn_banks[tile, n][:],
                        lhsT=c_words[:, b, g, j, :].bitcast(FP8X4),
                        lhsT_scale=c_scales[:, b, g, j, :],
                        rhs=wo_words[:, g, cols].bitcast(FP8X4),
                        rhs_scale=wo_scales[:, g, cols],
                        start=(g == 0),
                        stop=(g == PASSES - 1),
                    )

        def add_residual(tile):
            b, j = divmod(tile, POS)
            x1 = x1_tiles[tile]
            for n in range(DIM // BANK):
                cols = slice(n * BANK, (n + 1) * BANK)
                nc.vector.tensor_tensor(out=x1[:, cols], in0=attn_banks[tile, n][:], in1=x1[:, cols], op=ALU.add)
            nc.sync.dma_start(out=out0_view[:, j, b, :], in_=x1[:])

        mean_sq = const.tile([P, TILES], F32)
        mean_sq_eps = const.tile([P, TILES], F32)
        inv_rms = const.tile([P, TILES], F32)

        def inverse_rms(tile):
            col = slice(tile, tile + 1)
            squares = stream.tile([P, DIM], BF16, bufs=2)
            nc.scalar.activation(
                out=squares[:], in_=x1_tiles[tile][:], func=ACT.Square, scale=DIM**-0.5, accum_out=mean_sq[:, col]
            )
            nc.gpsimd.tensor_scalar(
                out=mean_sq_eps[:, col], in0=mean_sq[:, col], scalar1=EPS, scalar2=1.0, op0=ALU.add, op1=ALU.mult
            )
            nc.gpsimd.tensor_tensor(out=inv_rms[:, col], in0=mean_sq_eps[:, col], in1=minus_half[:], op=ALU.pow)

        m_tiles = {}

        def normalise(tile):
            m_tiles[tile] = stream.tile([P, 2, DIM // 2], BF16, name="m_%d" % tile, tag="m")
            x1_planes = x1_tiles[tile][:].rearrange("p (w e) -> p e w", e=2)
            w2_planes = w2_all.rearrange("p (w e) -> p e w", e=2)
            for e in range(2):
                nc.vector.scalar_tensor_tensor(
                    out=m_tiles[tile][:, e, :],
                    in0=x1_planes[:, e, :],
                    scalar=inv_rms[:, tile : tile + 1],
                    in1=w2_planes[:, e, :],
                    op0=ALU.mult,
                    op1=ALU.mult,
                )

        m_banks = {}

        def transpose_m(tile):
            m_banks[tile] = psum.tile([P, PASSES, PACK, P], BF16, tag="bank", name="m_bank_%d" % tile)
            for g in range(PASSES):
                for u in range(HALVES):
                    for e in range(2):
                        first = (HALVES * g + u) * P
                        nc.tensor.transpose(
                            m_banks[tile][:, g, 2 * u + e, :], m_tiles[tile][:, e, first : first + P], ident_bf16[:]
                        )

        grouped_m = {}

        def copy_out_m(tile):
            grouped_m[tile] = stream.tile(
                [P, PASSES * P * PACK], BF16, align_bytes=64, name="grouped_m_%d" % tile, tag="grouped_m"
            )
            nc.scalar.copy(
                out=grouped_m[tile][:].rearrange("p (g r v) -> p g r v", g=PASSES, v=PACK),
                in_=m_banks[tile][:].rearrange("p g v r -> p g r v"),
            )

        def quantise_m(tile):
            nc.vector.quantize_mx(
                out=m_words[:, tile, :, :].rearrange("p g r -> p (g r)").bitcast(FP8X4),
                scales=m_scales[:, tile, :, :].rearrange("p g r -> p (g r)"),
                in_=grouped_m[tile][:],
            )

        up_banks = {}

        def up_project(tile):
            for n in range(FF // BANK):
                cols = slice(n * BANK, (n + 1) * BANK)
                up_banks[tile, n] = psum.tile([P, BANK], F32, tag="bank", name="up_%d_%d" % (tile, n))
                for g in range(PASSES):
                    nc.tensor.matmul_mx(
                        out=up_banks[tile, n][:],
                        lhsT=m_words[:, tile, g, :].bitcast(FP8X4),
                        lhsT_scale=m_scales[:, tile, g, :],
                        rhs=w1_words[:, g, cols].bitcast(FP8X4),
                        rhs_scale=w1_scales[:, g, cols],
                        start=(g == 0),
                        stop=(g == PASSES - 1),
                    )

        g_tiles = {}

        def add_b1(tile):
            g_tiles[tile] = stream.tile([P, FF], F32, name="g_%d" % tile, tag="g")
            for n in range(FF // BANK):
                cols = slice(n * BANK, (n + 1) * BANK)
                nc.vector.tensor_tensor(
                    out=g_tiles[tile][:, cols], in0=up_banks[tile, n][:], in1=b1_all[:, cols], op=ALU.add
                )

        def gelu_and_store(tile, half):
            b, j = divmod(tile, POS)
            for n in (2 * half, 2 * half + 1):
                cols = slice(n * BANK, (n + 1) * BANK)
                nc.scalar.activation(out=g_tiles[tile][:, cols], in_=g_tiles[tile][:, cols], func=ACT.Gelu)
            cols = slice(half * FF // 2, (half + 1) * FF // 2)
            nc.sync.dma_start(out=out1_view[:, j, b, cols], in_=g_tiles[tile][:, cols])

        token_units = [token_unit(0, g) for g in range(PASSES)]
        token_grouped = [copy_out_unit(transpose_unit(unit)) for unit in token_units]
        for row in range(BO_ROWS + W2_ROWS):
            spread_row(row)
        for unit, grouped in zip(token_units, token_grouped):
            quantise_unit(unit, grouped)
        wo_units = [weight_unit(wo_raw, wo_words, wo_scales, chunk, g) for chunk in range(2) for g in range(PASSES)]
        wo_grouped = []
        for i in range(len(wo_units)):
            wo_grouped.append(copy_out_unit(transpose_unit(wo_units[i])))
            add_bias_to_x(i)
            if i > 0:
                quantise_unit(wo_units[i - 1], wo_grouped[i - 1])
        quantise_unit(wo_units[-1], wo_grouped[-1])
        project(0)

        units = [weight_unit(w1_raw, w1_words, w1_scales, 0, g) for g in range(PASSES)]
        units += [token_unit(1, g) for g in range(PASSES)]
        units += [weight_unit(w1_raw, w1_words, w1_scales, chunk, g) for chunk in (1, 2, 3) for g in range(PASSES)]
        unit_rounds = (len(units) + UNITS_PER_ROUND - 1) // UNITS_PER_ROUND
        first_up_round = unit_rounds + 1
        unit_grouped = {}
        for rnd in range(first_up_round + TILES + 1):
            up = rnd - first_up_round
            now = [i for i in range(rnd * UNITS_PER_ROUND, (rnd + 1) * UNITS_PER_ROUND) if i < len(units)]
            before = [i for i in range((rnd - 1) * UNITS_PER_ROUND, rnd * UNITS_PER_ROUND) if 0 <= i < len(units)]
            if 0 <= up < TILES:
                up_project(up)
            unit_banks = {}
            for i in now:
                unit_banks[i] = transpose_unit(units[i])
            if rnd < TILES:
                add_residual(rnd)
            if 1 <= rnd <= TILES:
                normalise(rnd - 1)
            if 2 <= rnd <= TILES + 1:
                copy_out_m(rnd - 2)
                quantise_m(rnd - 2)
            if 1 <= up <= TILES:
                gelu_and_store(up - 1, 0)
            for i in now[:1]:
                unit_grouped[i] = copy_out_unit(unit_banks[i])
            if rnd < TILES:
                inverse_rms(rnd)
            if 1 <= up <= TILES:
                gelu_and_store(up - 1, 1)
            for i in now[1:]:
                unit_grouped[i] = copy_out_unit(unit_banks[i])
            if 0 <= up < TILES:
                add_b1(up)
            for i in before:
                quantise_unit(units[i], unit_grouped[i])
            if rnd + 1 < TILES:
                project(rnd + 1)
            if 1 <= rnd <= TILES:
                transpose_m(rnd - 1)
            if rnd == unit_rounds - 1:
                for row in range(BO_ROWS + W2_ROWS, BO_ROWS + W2_ROWS + B1_ROWS):
                    spread_row(row)
            if 1 <= rnd <= POS:
                add_bias_to_x(rnd + POS - 1)
